import numpy as np
import ml_dtypes


def mxq(x, axis, fmt="e4m3"):
    dtype, down = {"e4m3": (ml_dtypes.float8_e4m3fn, 7), "e5m2": (ml_dtypes.float8_e5m2, 14)}[fmt]
    v = np.moveaxis(np.asarray(x, np.float32).astype(ml_dtypes.bfloat16).astype(np.float64), axis, -1)
    blocks = v.reshape(v.shape[:-1] + (-1, 32))
    amax = np.abs(blocks).max(-1, keepdims=True)
    byte = np.maximum(np.where(amax > 0, np.frexp(amax)[1] - 1 + 127, 0) - down, 1)
    scale = np.exp2(byte - 127.0)
    codes = (blocks / scale).astype(np.float32).astype(dtype).astype(np.float64)
    return np.moveaxis((codes * scale).reshape(v.shape), -1, axis)


WIDE = False


def mx_kscale(k):
    if not WIDE:
        return np.ones(k)
    levels = np.array([20, -20, 10, -10, 0])
    a = np.random.permutation(np.resize(levels, k // 512 * 4)).reshape(k // 512, 4)
    idx = np.arange(k)
    return np.exp2(a[idx // 512, idx % 128 // 32])


BF16 = ml_dtypes.bfloat16


def bf(x):
    return np.asarray(x, np.float32).astype(BF16)


def f64(x):
    return np.asarray(x).astype(np.float64)


B, MI, MO, NL = 512, 512, 512, 4
IR_DIMS = tuple(2 * l + 1 for l in range(NL))
FLAT_IN = MI * sum(IR_DIMS)
FLAT_OUT = MO * sum(IR_DIMS)


def setup_inputs():
    u = mx_kscale(MO)
    ug = np.concatenate([np.repeat(u, d) for d in IR_DIMS])
    inp = {"x": bf(np.random.standard_normal((B, FLAT_IN)))}
    for l in range(NL):
        inp["W%d" % l] = bf(np.random.standard_normal((MO, MI)) / np.sqrt(MI) / u[:, None])
    inp["bias"] = bf(np.random.standard_normal(MO))
    g = np.random.standard_normal((B, FLAT_OUT)) * np.exp2(np.random.randint(-12, 1, (B, 1))) * 4.0 * ug
    inp["grad_out"] = bf(g)
    return inp


def reference(x, W0, W1, W2, W3, bias, grad_out):
    g = f64(grad_out)
    outs = []
    start = 0
    for d, W in zip(IR_DIMS, (W0, W1, W2, W3)):
        seg = g[:, start:start + MO * d].reshape(B, MO, d)
        rows = seg.transpose(0, 2, 1).reshape(B * d, MO)
        gx = mxq(rows, 1, "e5m2") @ mxq(f64(W), 0, "e4m3")
        outs.append(gx.reshape(B, d, MI).transpose(0, 2, 1).reshape(B, MI * d))
        start += MO * d
    return np.concatenate(outs, axis=1)

@@ -1,0 +1,147 @@
+from contextlib import ExitStack
+
+import concourse.mybir as mybir
+from concourse.masks import make_identity
+
+BF16 = mybir.dt.bfloat16
+F32 = mybir.dt.float32
+U32 = mybir.dt.uint32
+U8 = mybir.dt.uint8
+E5M2_X4 = mybir.dt.float8_e5m2_x4
+E4M3_X4 = mybir.dt.float8_e4m3fn_x4
+
+P = 128
+PACK = 4
+ROWS = 512
+CH = 512
+IR_DIMS = (1, 3, 5, 7)
+SEG_START = (0, 512, 2048, 4608)
+ROW_BLOCKS = ROWS // P
+MAX_D = 7
+
+FLOPS = 2 * ROWS * sum(IR_DIMS) * CH * CH
+BYTES = 2 * ROWS * CH * sum(IR_DIMS) + 2 * len(IR_DIMS) * CH * CH + 4 * ROWS * CH * sum(IR_DIMS)
+
+
+def tile_so3_linear_pa_kernel(tc, x, W0, W1, W2, W3, bias, grad_out, out):
+    nc = tc.nc
+    weights = (W0, W1, W2, W3)
+
+    units = []
+    for rb in range(ROW_BLOCKS):
+        order = range(len(IR_DIMS)) if rb % 2 == 0 else reversed(range(len(IR_DIMS)))
+        units.extend((rb, l) for l in order)
+
+    with ExitStack() as ctx:
+        const = ctx.enter_context(tc.tile_pool(name="const", bufs=1))
+        resident = ctx.enter_context(tc.tile_pool(name="resident", bufs=1))
+        w_stage = ctx.enter_context(tc.tile_pool(name="w_stage", bufs=2))
+        work = ctx.enter_context(tc.tile_pool(name="work", bufs=2))
+        results = ctx.enter_context(tc.tile_pool(name="results", bufs=3))
+        psum_t = ctx.enter_context(tc.psum_pool(name="psum_t", bufs=3))
+        psum_acc = ctx.enter_context(tc.psum_pool(name="psum_acc", bufs=4))
+
+        identity = const.tile([P, P], F32)
+        make_identity(nc, identity[:])
+
+        g_raw = {}
+        w_raw = {}
+        for rb, l in units:
+            d = IR_DIMS[l]
+            g_raw[rb, l] = resident.tile([P, CH * d], BF16, name="g_raw_%d_%d" % (rb, l))
+            nc.sync.dma_start(
+                out=g_raw[rb, l][:],
+                in_=grad_out[rb * P : (rb + 1) * P, SEG_START[l] : SEG_START[l] + CH * d],
+            )
+            if rb == 0:
+                w_raw[l] = resident.tile([P, PACK, CH], BF16, name="w_raw_%d" % l)
+                nc.sync.dma_start(
+                    out=w_raw[l][:].rearrange("q (u e) m -> q u (e m)", u=2),
+                    in_=weights[l].rearrange("(u q e) m -> q u (e m)", u=2, e=2),
+                )
+
+        w_codes = {}
+        w_scales = {}
+
+        def quantise_weight(l):
+            w_grouped = w_stage.tile([P, CH, PACK], BF16, align_bytes=64)
+            nc.scalar.copy(out=w_grouped[:], in_=w_raw[l][:].rearrange("q t m -> q m t"))
+            w_codes[l] = resident.tile([P, CH], U32, name="w_codes_%d" % l, align_bytes=64)
+            w_scales[l] = resident.tile([P, CH], U8, name="w_scales_%d" % l, align_bytes=64)
+            nc.vector.quantize_mx(
+                out=w_codes[l][:].bitcast(E4M3_X4),
+                scales=w_scales[l][:],
+                in_=w_grouped[:].rearrange("q m t -> q (m t)"),
+            )
+
+        for rb, l in units:
+            d = IR_DIMS[l]
+            if rb == 0:
+                quantise_weight(l)
+
+            if d == 1:
+                planes = g_raw[rb, l][:].rearrange("b (i n) -> b i n", i=1)
+            else:
+                sorted_g = work.tile([P, MAX_D, CH], BF16, tag="sorted_g")
+                planes = sorted_g[:, 0:d, :]
+                nc.vector.tensor_copy(
+                    out=planes.rearrange("b i (h n) -> b h i n", h=2),
+                    in_=g_raw[rb, l][:].rearrange("b (h n i) -> b h i n", h=2, i=d),
+                )
+
+            grouped = work.tile([P, MAX_D, P, PACK], BF16, tag="grouped", align_bytes=64)
+            grouped_words = grouped[:].bitcast(F32)
+            for first in range(0, d, 2):
+                count = min(2, d - first)
+                flipped = psum_t.tile([P, 2, 2, P], F32, tag="flipped")
+                for k in range(count):
+                    words = planes[:, first + k, :].bitcast(F32)
+                    for u in range(2):
+                        nc.tensor.transpose(
+                            flipped[:, k, u, :], words[:, u * P : (u + 1) * P], identity[:]
+                        )
+                nc.scalar.copy(
+                    out=grouped_words[:, first : first + count, :, :],
+                    in_=flipped[:, 0:count, :, :].rearrange("q i u b -> q i b u"),
+                )
+
+            g_codes = work.tile([P, MAX_D * P], U32, tag="g_codes", align_bytes=64)
+            g_scales = work.tile([P, MAX_D * P], U8, tag="g_scales", align_bytes=64)
+            for i in range(d):
+                cols = slice(i * P, (i + 1) * P)
+                nc.vector.quantize_mx(
+                    out=g_codes[:, cols].bitcast(E5M2_X4),
+                    scales=g_scales[:, cols],
+                    in_=grouped[:, i, :, :].rearrange("q b t -> q (b t)"),
+                )
+
+            woven = results.tile([P, CH * MAX_D], F32, tag="woven")
+            if d > 1:
+                product = work.tile([P, MAX_D, CH], F32, tag="product")
+            for i in range(d):
+                cols = slice(i * P, (i + 1) * P)
+                acc = psum_acc.tile([P, CH], F32, tag="acc")
+                nc.tensor.matmul_mx(
+                    out=acc[:],
+                    lhsT=g_codes[:, cols].bitcast(E5M2_X4),
+                    lhsT_scale=g_scales[:, cols],
+                    rhs=w_codes[l][:].bitcast(E4M3_X4),
+                    rhs_scale=w_scales[l][:],
+                    start=True,
+                    stop=True,
+                )
+                if d == 1:
+                    nc.scalar.copy(out=woven[:, 0:CH], in_=acc[:])
+                else:
+                    nc.scalar.copy(out=product[:, i, :], in_=acc[:])
+
+            if d > 1:
+                nc.vector.tensor_copy(
+                    out=woven[:, 0 : CH * d].rearrange("b (m i) -> b m i", i=d),
+                    in_=product[:, 0:d, :].rearrange("b i m -> b m i"),
+                )
+
+            nc.sync.dma_start(
+                out=out[rb * P : (rb + 1) * P, SEG_START[l] : SEG_START[l] + CH * d],
+                in_=woven[:, 0 : CH * d],
+            )

@@ -18,6 +18,7 @@ IR_DIMS = (1, 3, 5, 7)
 SEG_START = (0, 512, 2048, 4608)
 ROW_BLOCKS = ROWS // P
 MAX_D = 7
+MAX_OPEN = 4
 
 FLOPS = 2 * ROWS * sum(IR_DIMS) * CH * CH
 BYTES = 2 * ROWS * CH * sum(IR_DIMS) + 2 * len(IR_DIMS) * CH * CH + 4 * ROWS * CH * sum(IR_DIMS)
@@ -84,10 +85,13 @@ def tile_so3_linear_pa_kernel(tc, x, W0, W1, W2, W3, bias, grad_out, out):
             else:
                 sorted_g = work.tile([P, MAX_D, CH], BF16, tag="sorted_g")
                 planes = sorted_g[:, 0:d, :]
-                nc.vector.tensor_copy(
-                    out=planes.rearrange("b i (h n) -> b h i n", h=2),
-                    in_=g_raw[rb, l][:].rearrange("b (h n i) -> b h i n", h=2, i=d),
-                )
+                mixed = g_raw[rb, l][:].rearrange("b (n i) -> b n i", i=d)
+                for first in range(0, d, MAX_OPEN):
+                    last = min(first + MAX_OPEN, d)
+                    nc.vector.tensor_copy(
+                        out=planes[:, first:last, :].rearrange("b i n -> b n i"),
+                        in_=mixed[:, :, first:last],
+                    )
 
             grouped = work.tile([P, MAX_D, P, PACK], BF16, tag="grouped", align_bytes=64)
             grouped_words = grouped[:].bitcast(F32)
@@ -137,8 +141,8 @@ def tile_so3_linear_pa_kernel(tc, x, W0, W1, W2, W3, bias, grad_out, out):
 
             if d > 1:
                 nc.vector.tensor_copy(
-                    out=woven[:, 0 : CH * d].rearrange("b (m i) -> b m i", i=d),
-                    in_=product[:, 0:d, :].rearrange("b i m -> b m i"),
+                    out=woven[:, 0 : CH * d].rearrange("b (c j i) -> b c i j", j=2, i=d),
+                    in_=product[:, 0:d, :].rearrange("b i (c j) -> b c i j", j=2),
                 )
 
             nc.sync.dma_start(

@@ -28,10 +28,7 @@ def tile_so3_linear_pa_kernel(tc, x, W0, W1, W2, W3, bias, grad_out, out):
     nc = tc.nc
     weights = (W0, W1, W2, W3)
 
-    units = []
-    for rb in range(ROW_BLOCKS):
-        order = range(len(IR_DIMS)) if rb % 2 == 0 else reversed(range(len(IR_DIMS)))
-        units.extend((rb, l) for l in order)
+    units = [(rb, l) for l in reversed(range(len(IR_DIMS))) for rb in range(ROW_BLOCKS)]
 
     with ExitStack() as ctx:
         const = ctx.enter_context(tc.tile_pool(name="const", bufs=1))
@@ -63,10 +60,19 @@ def tile_so3_linear_pa_kernel(tc, x, W0, W1, W2, W3, bias, grad_out, out):
 
         w_codes = {}
         w_scales = {}
+        planes = {}
+        grouped = {}
+        g_codes = {}
+        g_scales = {}
+        product = {}
+        woven = {}
 
         def quantise_weight(l):
             w_grouped = w_stage.tile([P, CH, PACK], BF16, align_bytes=64)
-            nc.scalar.copy(out=w_grouped[:], in_=w_raw[l][:].rearrange("q t m -> q m t"))
+            nc.vector.tensor_copy(
+                out=w_grouped[:].rearrange("q (c j) t -> q c t j", j=4),
+                in_=w_raw[l][:].rearrange("q t (c j) -> q c t j", j=4),
+            )
             w_codes[l] = resident.tile([P, CH], U32, name="w_codes_%d" % l, align_bytes=64)
             w_scales[l] = resident.tile([P, CH], U8, name="w_scales_%d" % l, align_bytes=64)
             nc.vector.quantize_mx(
@@ -75,77 +81,108 @@ def tile_so3_linear_pa_kernel(tc, x, W0, W1, W2, W3, bias, grad_out, out):
                 in_=w_grouped[:].rearrange("q m t -> q (m t)"),
             )
 
-        for rb, l in units:
-            d = IR_DIMS[l]
-            if rb == 0:
-                quantise_weight(l)
-
+        def sort(unit):
+            d = IR_DIMS[unit[1]]
             if d == 1:
-                planes = g_raw[rb, l][:].rearrange("b (i n) -> b i n", i=1)
-            else:
-                sorted_g = work.tile([P, MAX_D, CH], BF16, tag="sorted_g")
-                planes = sorted_g[:, 0:d, :]
-                mixed = g_raw[rb, l][:].rearrange("b (n i) -> b n i", i=d)
-                for first in range(0, d, MAX_OPEN):
-                    last = min(first + MAX_OPEN, d)
-                    nc.vector.tensor_copy(
-                        out=planes[:, first:last, :].rearrange("b i n -> b n i"),
-                        in_=mixed[:, :, first:last],
-                    )
+                planes[unit] = g_raw[unit][:].rearrange("b (i n) -> b i n", i=1)
+                return
+            sorted_g = work.tile([P, MAX_D, CH], BF16, tag="sorted_g")
+            planes[unit] = sorted_g[:, 0:d, :]
+            mixed = g_raw[unit][:].rearrange("b (n i) -> b n i", i=d)
+            for lo in range(0, d, MAX_OPEN):
+                hi = min(lo + MAX_OPEN, d)
+                nc.vector.tensor_copy(
+                    out=sorted_g[:, lo:hi, :].rearrange("b i n -> b n i"),
+                    in_=mixed[:, :, lo:hi],
+                )
 
-            grouped = work.tile([P, MAX_D, P, PACK], BF16, tag="grouped", align_bytes=64)
-            grouped_words = grouped[:].bitcast(F32)
-            for first in range(0, d, 2):
-                count = min(2, d - first)
+        def flip(unit):
+            d = IR_DIMS[unit[1]]
+            grouped[unit] = work.tile(
+                [P, MAX_D, P, PACK], BF16, tag="grouped", name="grouped", align_bytes=64
+            )
+            grouped_words = grouped[unit][:].bitcast(F32)
+            for lo in range(0, d, 2):
+                count = min(2, d - lo)
                 flipped = psum_t.tile([P, 2, 2, P], F32, tag="flipped")
                 for k in range(count):
-                    words = planes[:, first + k, :].bitcast(F32)
+                    words = planes[unit][:, lo + k, :].bitcast(F32)
                     for u in range(2):
                         nc.tensor.transpose(
                             flipped[:, k, u, :], words[:, u * P : (u + 1) * P], identity[:]
                         )
                 nc.scalar.copy(
-                    out=grouped_words[:, first : first + count, :, :],
+                    out=grouped_words[:, lo : lo + count, :, :],
                     in_=flipped[:, 0:count, :, :].rearrange("q i u b -> q i b u"),
                 )
 
-            g_codes = work.tile([P, MAX_D * P], U32, tag="g_codes", align_bytes=64)
-            g_scales = work.tile([P, MAX_D * P], U8, tag="g_scales", align_bytes=64)
+        def quantise(unit):
+            d = IR_DIMS[unit[1]]
+            g_codes[unit] = work.tile(
+                [P, MAX_D * P], U32, tag="g_codes", name="g_codes", align_bytes=64
+            )
+            g_scales[unit] = work.tile(
+                [P, MAX_D * P], U8, tag="g_scales", name="g_scales", align_bytes=64
+            )
             for i in range(d):
                 cols = slice(i * P, (i + 1) * P)
                 nc.vector.quantize_mx(
-                    out=g_codes[:, cols].bitcast(E5M2_X4),
-                    scales=g_scales[:, cols],
-                    in_=grouped[:, i, :, :].rearrange("q b t -> q (b t)"),
+                    out=g_codes[unit][:, cols].bitcast(E5M2_X4),
+                    scales=g_scales[unit][:, cols],
+                    in_=grouped[unit][:, i, :, :].rearrange("q b t -> q (b t)"),
                 )
 
-            woven = results.tile([P, CH * MAX_D], F32, tag="woven")
-            if d > 1:
-                product = work.tile([P, MAX_D, CH], F32, tag="product")
+        def multiply(unit):
+            l = unit[1]
+            d = IR_DIMS[l]
+            if d == 1:
+                woven[unit] = results.tile([P, CH], F32, tag="plain", name="plain", bufs=ROW_BLOCKS)
+            else:
+                woven[unit] = results.tile([P, CH * MAX_D], F32, tag="woven", name="woven")
+                product[unit] = work.tile([P, MAX_D, CH], F32, tag="product", name="product")
             for i in range(d):
                 cols = slice(i * P, (i + 1) * P)
                 acc = psum_acc.tile([P, CH], F32, tag="acc")
                 nc.tensor.matmul_mx(
                     out=acc[:],
-                    lhsT=g_codes[:, cols].bitcast(E5M2_X4),
-                    lhsT_scale=g_scales[:, cols],
+                    lhsT=g_codes[unit][:, cols].bitcast(E5M2_X4),
+                    lhsT_scale=g_scales[unit][:, cols],
                     rhs=w_codes[l][:].bitcast(E4M3_X4),
                     rhs_scale=w_scales[l][:],
                     start=True,
                     stop=True,
                 )
                 if d == 1:
-                    nc.scalar.copy(out=woven[:, 0:CH], in_=acc[:])
+                    nc.scalar.copy(out=woven[unit][:, 0:CH], in_=acc[:])
                 else:
-                    nc.scalar.copy(out=product[:, i, :], in_=acc[:])
+                    nc.scalar.copy(out=product[unit][:, i, :], in_=acc[:])
 
+        def weave_and_store(unit):
+            rb, l = unit
+            d = IR_DIMS[l]
             if d > 1:
                 nc.vector.tensor_copy(
-                    out=woven[:, 0 : CH * d].rearrange("b (c j i) -> b c i j", j=2, i=d),
-                    in_=product[:, 0:d, :].rearrange("b i (c j) -> b c i j", j=2),
+                    out=woven[unit][:, 0 : CH * d].rearrange("b (c j i) -> b c i j", j=2, i=d),
+                    in_=product[unit][:, 0:d, :].rearrange("b i (c j) -> b c i j", j=2),
                 )
-
             nc.sync.dma_start(
                 out=out[rb * P : (rb + 1) * P, SEG_START[l] : SEG_START[l] + CH * d],
-                in_=woven[:, 0 : CH * d],
+                in_=woven[unit][:, 0 : CH * d],
             )
+
+        n_units = len(units)
+        with tc.manual_schedule():
+            sort(units[0])
+            for r in range(n_units + 2):
+                if 1 <= r <= n_units:
+                    quantise(units[r - 1])
+                if r < n_units and units[r][0] == 0:
+                    quantise_weight(units[r][1])
+                if r < n_units:
+                    flip(units[r])
+                if 1 <= r <= n_units:
+                    multiply(units[r - 1])
+                if r + 1 < n_units:
+                    sort(units[r + 1])
+                if r >= 2:
+                    weave_and_store(units[r - 2])

@@ -16,30 +16,31 @@ ROWS = 512
 CH = 512
 IR_DIMS = (1, 3, 5, 7)
 SEG_START = (0, 512, 2048, 4608)
+N_SEG = len(IR_DIMS)
 ROW_BLOCKS = ROWS // P
-MAX_D = 7
+MAX_D = max(IR_DIMS)
 MAX_OPEN = 4
+BANK_PLANES = 2
 
 FLOPS = 2 * ROWS * sum(IR_DIMS) * CH * CH
-BYTES = 2 * ROWS * CH * sum(IR_DIMS) + 2 * len(IR_DIMS) * CH * CH + 4 * ROWS * CH * sum(IR_DIMS)
+BYTES = (2 + 4) * ROWS * CH * sum(IR_DIMS) + 2 * N_SEG * CH * CH
 
 
 def tile_so3_linear_pa_kernel(tc, x, W0, W1, W2, W3, bias, grad_out, out):
     nc = tc.nc
     weights = (W0, W1, W2, W3)
 
-    units = [(rb, l) for l in reversed(range(len(IR_DIMS))) for rb in range(ROW_BLOCKS)]
+    units = [(rb, l) for l in reversed(range(N_SEG)) for rb in range(ROW_BLOCKS)]
+    n_units = len(units)
 
     with ExitStack() as ctx:
-        const = ctx.enter_context(tc.tile_pool(name="const", bufs=1))
         resident = ctx.enter_context(tc.tile_pool(name="resident", bufs=1))
-        w_stage = ctx.enter_context(tc.tile_pool(name="w_stage", bufs=2))
         work = ctx.enter_context(tc.tile_pool(name="work", bufs=2))
         results = ctx.enter_context(tc.tile_pool(name="results", bufs=3))
-        psum_t = ctx.enter_context(tc.psum_pool(name="psum_t", bufs=3))
-        psum_acc = ctx.enter_context(tc.psum_pool(name="psum_acc", bufs=4))
+        psum_flip = ctx.enter_context(tc.psum_pool(name="psum_flip", bufs=3))
+        psum_acc = ctx.enter_context(tc.psum_pool(name="psum_acc", bufs=5))
 
-        identity = const.tile([P, P], F32)
+        identity = resident.tile([P, P], F32)
         make_identity(nc, identity[:])
 
         g_raw = {}
@@ -58,6 +59,7 @@ def tile_so3_linear_pa_kernel(tc, x, W0, W1, W2, W3, bias, grad_out, out):
                     in_=weights[l].rearrange("(u q e) m -> q u (e m)", u=2, e=2),
                 )
 
+        w_grouped = {}
         w_codes = {}
         w_scales = {}
         planes = {}
@@ -65,20 +67,22 @@ def tile_so3_linear_pa_kernel(tc, x, W0, W1, W2, W3, bias, grad_out, out):
         g_codes = {}
         g_scales = {}
         product = {}
-        woven = {}
+        result = {}
 
-        def quantise_weight(l):
-            w_grouped = w_stage.tile([P, CH, PACK], BF16, align_bytes=64)
+        def group_weight(l):
+            w_grouped[l] = work.tile([P, CH, PACK], BF16, tag="w_grouped", name="w_grouped", align_bytes=64)
             nc.vector.tensor_copy(
-                out=w_grouped[:].rearrange("q (c j) t -> q c t j", j=4),
+                out=w_grouped[l][:].rearrange("q (c j) t -> q c t j", j=4),
                 in_=w_raw[l][:].rearrange("q t (c j) -> q c t j", j=4),
             )
+
+        def quantise_weight(l):
             w_codes[l] = resident.tile([P, CH], U32, name="w_codes_%d" % l, align_bytes=64)
             w_scales[l] = resident.tile([P, CH], U8, name="w_scales_%d" % l, align_bytes=64)
             nc.vector.quantize_mx(
                 out=w_codes[l][:].bitcast(E4M3_X4),
                 scales=w_scales[l][:],
-                in_=w_grouped[:].rearrange("q m t -> q (m t)"),
+                in_=w_grouped[l][:].rearrange("q m t -> q (m t)"),
             )
 
         def sort(unit):
@@ -89,8 +93,10 @@ def tile_so3_linear_pa_kernel(tc, x, W0, W1, W2, W3, bias, grad_out, out):
             sorted_g = work.tile([P, MAX_D, CH], BF16, tag="sorted_g")
             planes[unit] = sorted_g[:, 0:d, :]
             mixed = g_raw[unit][:].rearrange("b (n i) -> b n i", i=d)
-            for lo in range(0, d, MAX_OPEN):
-                hi = min(lo + MAX_OPEN, d)
+            n_deals = -(-d // MAX_OPEN)
+            share = -(-d // n_deals)
+            for lo in range(0, d, share):
+                hi = min(lo + share, d)
                 nc.vector.tensor_copy(
                     out=sorted_g[:, lo:hi, :].rearrange("b i n -> b n i"),
                     in_=mixed[:, :, lo:hi],
@@ -98,19 +104,15 @@ def tile_so3_linear_pa_kernel(tc, x, W0, W1, W2, W3, bias, grad_out, out):
 
         def flip(unit):
             d = IR_DIMS[unit[1]]
-            grouped[unit] = work.tile(
-                [P, MAX_D, P, PACK], BF16, tag="grouped", name="grouped", align_bytes=64
-            )
+            grouped[unit] = work.tile([P, MAX_D, P, PACK], BF16, tag="grouped", name="grouped", align_bytes=64)
             grouped_words = grouped[unit][:].bitcast(F32)
-            for lo in range(0, d, 2):
-                count = min(2, d - lo)
-                flipped = psum_t.tile([P, 2, 2, P], F32, tag="flipped")
+            for lo in range(0, d, BANK_PLANES):
+                count = min(BANK_PLANES, d - lo)
+                flipped = psum_flip.tile([P, BANK_PLANES, 2, P], F32, tag="flipped")
                 for k in range(count):
                     words = planes[unit][:, lo + k, :].bitcast(F32)
                     for u in range(2):
-                        nc.tensor.transpose(
-                            flipped[:, k, u, :], words[:, u * P : (u + 1) * P], identity[:]
-                        )
+                        nc.tensor.transpose(flipped[:, k, u, :], words[:, u * P : (u + 1) * P], identity[:])
                 nc.scalar.copy(
                     out=grouped_words[:, lo : lo + count, :, :],
                     in_=flipped[:, 0:count, :, :].rearrange("q i u b -> q i b u"),
@@ -118,12 +120,8 @@ def tile_so3_linear_pa_kernel(tc, x, W0, W1, W2, W3, bias, grad_out, out):
 
         def quantise(unit):
             d = IR_DIMS[unit[1]]
-            g_codes[unit] = work.tile(
-                [P, MAX_D * P], U32, tag="g_codes", name="g_codes", align_bytes=64
-            )
-            g_scales[unit] = work.tile(
-                [P, MAX_D * P], U8, tag="g_scales", name="g_scales", align_bytes=64
-            )
+            g_codes[unit] = work.tile([P, MAX_D * P], U32, tag="g_codes", name="g_codes", align_bytes=64)
+            g_scales[unit] = work.tile([P, MAX_D * P], U8, tag="g_scales", name="g_scales", align_bytes=64)
             for i in range(d):
                 cols = slice(i * P, (i + 1) * P)
                 nc.vector.quantize_mx(
@@ -136,9 +134,10 @@ def tile_so3_linear_pa_kernel(tc, x, W0, W1, W2, W3, bias, grad_out, out):
             l = unit[1]
             d = IR_DIMS[l]
             if d == 1:
-                woven[unit] = results.tile([P, CH], F32, tag="plain", name="plain", bufs=ROW_BLOCKS)
+                result[unit] = results.tile([P, CH], F32, tag="plain", name="plain", bufs=ROW_BLOCKS)
+                product[unit] = result[unit][:].rearrange("b (i m) -> b i m", i=1)
             else:
-                woven[unit] = results.tile([P, CH * MAX_D], F32, tag="woven", name="woven")
+                result[unit] = results.tile([P, CH * MAX_D], F32, tag="woven", name="woven")
                 product[unit] = work.tile([P, MAX_D, CH], F32, tag="product", name="product")
             for i in range(d):
                 cols = slice(i * P, (i + 1) * P)
@@ -152,37 +151,36 @@ def tile_so3_linear_pa_kernel(tc, x, W0, W1, W2, W3, bias, grad_out, out):
                     start=True,
                     stop=True,
                 )
-                if d == 1:
-                    nc.scalar.copy(out=woven[unit][:, 0:CH], in_=acc[:])
-                else:
-                    nc.scalar.copy(out=product[unit][:, i, :], in_=acc[:])
+                nc.scalar.copy(out=product[unit][:, i, :], in_=acc[:])
 
         def weave_and_store(unit):
             rb, l = unit
             d = IR_DIMS[l]
             if d > 1:
                 nc.vector.tensor_copy(
-                    out=woven[unit][:, 0 : CH * d].rearrange("b (c j i) -> b c i j", j=2, i=d),
+                    out=result[unit][:, 0 : CH * d].rearrange("b (c j i) -> b c i j", j=2, i=d),
                     in_=product[unit][:, 0:d, :].rearrange("b i (c j) -> b c i j", j=2),
                 )
             nc.sync.dma_start(
                 out=out[rb * P : (rb + 1) * P, SEG_START[l] : SEG_START[l] + CH * d],
-                in_=woven[unit][:, 0 : CH * d],
+                in_=result[unit][:, 0 : CH * d],
             )
 
-        n_units = len(units)
         with tc.manual_schedule():
             sort(units[0])
             for r in range(n_units + 2):
+                new_weight = r < n_units and units[r][0] == 0
                 if 1 <= r <= n_units:
                     quantise(units[r - 1])
-                if r < n_units and units[r][0] == 0:
-                    quantise_weight(units[r][1])
+                if new_weight:
+                    group_weight(units[r][1])
                 if r < n_units:
                     flip(units[r])
                 if 1 <= r <= n_units:
                     multiply(units[r - 1])
                 if r + 1 < n_units:
                     sort(units[r + 1])
+                if new_weight:
+                    quantise_weight(units[r][1])
                 if r >= 2:
                     weave_and_store(units[r - 2])

@@ -122,13 +122,16 @@ def tile_so3_linear_pa_kernel(tc, x, W0, W1, W2, W3, bias, grad_out, out):
             d = IR_DIMS[unit[1]]
             g_codes[unit] = work.tile([P, MAX_D * P], U32, tag="g_codes", name="g_codes", align_bytes=64)
             g_scales[unit] = work.tile([P, MAX_D * P], U8, tag="g_scales", name="g_scales", align_bytes=64)
-            for i in range(d):
-                cols = slice(i * P, (i + 1) * P)
-                nc.vector.quantize_mx(
-                    out=g_codes[unit][:, cols].bitcast(E5M2_X4),
-                    scales=g_scales[unit][:, cols],
-                    in_=grouped[unit][:, i, :, :].rearrange("q b t -> q (b t)"),
-                )
+            lo = 0
+            for run in (4, 2, 1):
+                if d - lo >= run:
+                    cols = slice(lo * P, (lo + run) * P)
+                    nc.vector.quantize_mx(
+                        out=g_codes[unit][:, cols].bitcast(E5M2_X4),
+                        scales=g_scales[unit][:, cols],
+                        in_=grouped[unit][:, lo : lo + run, :, :].rearrange("q i b t -> q (i b t)"),
+                    )
+                    lo += run
 
         def multiply(unit):
             l = unit[1]

@@ -67,6 +67,7 @@ def tile_so3_linear_pa_kernel(tc, x, W0, W1, W2, W3, bias, grad_out, out):
         g_codes = {}
         g_scales = {}
         product = {}
+        left_over = []
         result = {}
 
         def group_weight(l):
@@ -154,7 +155,10 @@ def tile_so3_linear_pa_kernel(tc, x, W0, W1, W2, W3, bias, grad_out, out):
                     start=True,
                     stop=True,
                 )
-                nc.scalar.copy(out=product[unit][:, i, :], in_=acc[:])
+                if d == MAX_D and i == d - 1:
+                    left_over.append((product[unit][:, i, :], acc))
+                else:
+                    nc.scalar.copy(out=product[unit][:, i, :], in_=acc[:])
 
         def weave_and_store(unit):
             rb, l = unit
@@ -187,3 +191,6 @@ def tile_so3_linear_pa_kernel(tc, x, W0, W1, W2, W3, bias, grad_out, out):
                     quantise_weight(units[r][1])
                 if r >= 2:
                     weave_and_store(units[r - 2])
+                for plane, acc in left_over:
+                    nc.vector.tensor_copy(out=plane, in_=acc[:])
+                left_over.clear()

@@ -175,22 +175,22 @@ def tile_so3_linear_pa_kernel(tc, x, W0, W1, W2, W3, bias, grad_out, out):
 
         with tc.manual_schedule():
             sort(units[0])
-            for r in range(n_units + 2):
+            for r in range(n_units + 3):
                 new_weight = r < n_units and units[r][0] == 0
-                if 1 <= r <= n_units:
-                    quantise(units[r - 1])
                 if new_weight:
                     group_weight(units[r][1])
+                if 2 <= r < n_units + 2:
+                    multiply(units[r - 2])
+                if r >= 3:
+                    weave_and_store(units[r - 3])
+                if 1 <= r <= n_units:
+                    quantise(units[r - 1])
                 if r < n_units:
                     flip(units[r])
-                if 1 <= r <= n_units:
-                    multiply(units[r - 1])
                 if r + 1 < n_units:
                     sort(units[r + 1])
                 if new_weight:
                     quantise_weight(units[r][1])
-                if r >= 2:
-                    weave_and_store(units[r - 2])
                 for plane, acc in left_over:
                     nc.vector.tensor_copy(out=plane, in_=acc[:])
                 left_over.clear()

@@ -67,7 +67,6 @@ def tile_so3_linear_pa_kernel(tc, x, W0, W1, W2, W3, bias, grad_out, out):
         g_codes = {}
         g_scales = {}
         product = {}
-        left_over = []
         result = {}
 
         def group_weight(l):
@@ -155,10 +154,7 @@ def tile_so3_linear_pa_kernel(tc, x, W0, W1, W2, W3, bias, grad_out, out):
                     start=True,
                     stop=True,
                 )
-                if d == MAX_D and i == d - 1:
-                    left_over.append((product[unit][:, i, :], acc))
-                else:
-                    nc.scalar.copy(out=product[unit][:, i, :], in_=acc[:])
+                nc.scalar.copy(out=product[unit][:, i, :], in_=acc[:])
 
         def weave_and_store(unit):
             rb, l = unit
@@ -191,6 +187,3 @@ def tile_so3_linear_pa_kernel(tc, x, W0, W1, W2, W3, bias, grad_out, out):
                     sort(units[r + 1])
                 if new_weight:
                     quantise_weight(units[r][1])
-                for plane, acc in left_over:
-                    nc.vector.tensor_copy(out=plane, in_=acc[:])
-                left_over.clear()

from contextlib import ExitStack

import concourse.mybir as mybir
from concourse.masks import make_identity

BF16 = mybir.dt.bfloat16
F32 = mybir.dt.float32
U32 = mybir.dt.uint32
U8 = mybir.dt.uint8
E5M2_X4 = mybir.dt.float8_e5m2_x4
E4M3_X4 = mybir.dt.float8_e4m3fn_x4

P = 128
PACK = 4
ROWS = 512
CH = 512
IR_DIMS = (1, 3, 5, 7)
SEG_START = (0, 512, 2048, 4608)
N_SEG = len(IR_DIMS)
ROW_BLOCKS = ROWS // P
MAX_D = max(IR_DIMS)
MAX_OPEN = 4
BANK_PLANES = 2

FLOPS = 2 * ROWS * sum(IR_DIMS) * CH * CH
BYTES = (2 + 4) * ROWS * CH * sum(IR_DIMS) + 2 * N_SEG * CH * CH


def tile_so3_linear_pa_kernel(tc, x, W0, W1, W2, W3, bias, grad_out, out):
    nc = tc.nc
    weights = (W0, W1, W2, W3)

    units = [(rb, l) for l in reversed(range(N_SEG)) for rb in range(ROW_BLOCKS)]
    n_units = len(units)

    with ExitStack() as ctx:
        resident = ctx.enter_context(tc.tile_pool(name="resident", bufs=1))
        work = ctx.enter_context(tc.tile_pool(name="work", bufs=2))
        results = ctx.enter_context(tc.tile_pool(name="results", bufs=3))
        psum_flip = ctx.enter_context(tc.psum_pool(name="psum_flip", bufs=3))
        psum_acc = ctx.enter_context(tc.psum_pool(name="psum_acc", bufs=5))

        identity = resident.tile([P, P], F32)
        make_identity(nc, identity[:])

        g_raw = {}
        w_raw = {}
        for rb, l in units:
            d = IR_DIMS[l]
            g_raw[rb, l] = resident.tile([P, CH * d], BF16, name="g_raw_%d_%d" % (rb, l))
            nc.sync.dma_start(
                out=g_raw[rb, l][:],
                in_=grad_out[rb * P : (rb + 1) * P, SEG_START[l] : SEG_START[l] + CH * d],
            )
            if rb == 0:
                w_raw[l] = resident.tile([P, PACK, CH], BF16, name="w_raw_%d" % l)
                nc.sync.dma_start(
                    out=w_raw[l][:].rearrange("q (u e) m -> q u (e m)", u=2),
                    in_=weights[l].rearrange("(u q e) m -> q u (e m)", u=2, e=2),
                )

        w_grouped = {}
        w_codes = {}
        w_scales = {}
        planes = {}
        grouped = {}
        g_codes = {}
        g_scales = {}
        product = {}
        result = {}

        def group_weight(l):
            w_grouped[l] = work.tile([P, CH, PACK], BF16, tag="w_grouped", name="w_grouped", align_bytes=64)
            nc.vector.tensor_copy(
                out=w_grouped[l][:].rearrange("q (c j) t -> q c t j", j=4),
                in_=w_raw[l][:].rearrange("q t (c j) -> q c t j", j=4),
            )

        def quantise_weight(l):
            w_codes[l] = resident.tile([P, CH], U32, name="w_codes_%d" % l, align_bytes=64)
            w_scales[l] = resident.tile([P, CH], U8, name="w_scales_%d" % l, align_bytes=64)
            nc.vector.quantize_mx(
                out=w_codes[l][:].bitcast(E4M3_X4),
                scales=w_scales[l][:],
                in_=w_grouped[l][:].rearrange("q m t -> q (m t)"),
            )

        def sort(unit):
            d = IR_DIMS[unit[1]]
            if d == 1:
                planes[unit] = g_raw[unit][:].rearrange("b (i n) -> b i n", i=1)
                return
            sorted_g = work.tile([P, MAX_D, CH], BF16, tag="sorted_g")
            planes[unit] = sorted_g[:, 0:d, :]
            mixed = g_raw[unit][:].rearrange("b (n i) -> b n i", i=d)
            n_deals = -(-d // MAX_OPEN)
            share = -(-d // n_deals)
            for lo in range(0, d, share):
                hi = min(lo + share, d)
                nc.vector.tensor_copy(
                    out=sorted_g[:, lo:hi, :].rearrange("b i n -> b n i"),
                    in_=mixed[:, :, lo:hi],
                )

        def flip(unit):
            d = IR_DIMS[unit[1]]
            grouped[unit] = work.tile([P, MAX_D, P, PACK], BF16, tag="grouped", name="grouped", align_bytes=64)
            grouped_words = grouped[unit][:].bitcast(F32)
            for lo in range(0, d, BANK_PLANES):
                count = min(BANK_PLANES, d - lo)
                flipped = psum_flip.tile([P, BANK_PLANES, 2, P], F32, tag="flipped")
                for k in range(count):
                    words = planes[unit][:, lo + k, :].bitcast(F32)
                    for u in range(2):
                        nc.tensor.transpose(flipped[:, k, u, :], words[:, u * P : (u + 1) * P], identity[:])
                nc.scalar.copy(
                    out=grouped_words[:, lo : lo + count, :, :],
                    in_=flipped[:, 0:count, :, :].rearrange("q i u b -> q i b u"),
                )

        def quantise(unit):
            d = IR_DIMS[unit[1]]
            g_codes[unit] = work.tile([P, MAX_D * P], U32, tag="g_codes", name="g_codes", align_bytes=64)
            g_scales[unit] = work.tile([P, MAX_D * P], U8, tag="g_scales", name="g_scales", align_bytes=64)
            lo = 0
            for run in (4, 2, 1):
                if d - lo >= run:
                    cols = slice(lo * P, (lo + run) * P)
                    nc.vector.quantize_mx(
                        out=g_codes[unit][:, cols].bitcast(E5M2_X4),
                        scales=g_scales[unit][:, cols],
                        in_=grouped[unit][:, lo : lo + run, :, :].rearrange("q i b t -> q (i b t)"),
                    )
                    lo += run

        def multiply(unit):
            l = unit[1]
            d = IR_DIMS[l]
            if d == 1:
                result[unit] = results.tile([P, CH], F32, tag="plain", name="plain", bufs=ROW_BLOCKS)
                product[unit] = result[unit][:].rearrange("b (i m) -> b i m", i=1)
            else:
                result[unit] = results.tile([P, CH * MAX_D], F32, tag="woven", name="woven")
                product[unit] = work.tile([P, MAX_D, CH], F32, tag="product", name="product")
            for i in range(d):
                cols = slice(i * P, (i + 1) * P)
                acc = psum_acc.tile([P, CH], F32, tag="acc")
                nc.tensor.matmul_mx(
                    out=acc[:],
                    lhsT=g_codes[unit][:, cols].bitcast(E5M2_X4),
                    lhsT_scale=g_scales[unit][:, cols],
                    rhs=w_codes[l][:].bitcast(E4M3_X4),
                    rhs_scale=w_scales[l][:],
                    start=True,
                    stop=True,
                )
                nc.scalar.copy(out=product[unit][:, i, :], in_=acc[:])

        def weave_and_store(unit):
            rb, l = unit
            d = IR_DIMS[l]
            if d > 1:
                nc.vector.tensor_copy(
                    out=result[unit][:, 0 : CH * d].rearrange("b (c j i) -> b c i j", j=2, i=d),
                    in_=product[unit][:, 0:d, :].rearrange("b i (c j) -> b c i j", j=2),
                )
            nc.sync.dma_start(
                out=out[rb * P : (rb + 1) * P, SEG_START[l] : SEG_START[l] + CH * d],
                in_=result[unit][:, 0 : CH * d],
            )

        with tc.manual_schedule():
            sort(units[0])
            for r in range(n_units + 3):
                new_weight = r < n_units and units[r][0] == 0
                if new_weight:
                    group_weight(units[r][1])
                if 2 <= r < n_units + 2:
                    multiply(units[r - 2])
                if r >= 3:
                    weave_and_store(units[r - 3])
                if 1 <= r <= n_units:
                    quantise(units[r - 1])
                if r < n_units:
                    flip(units[r])
                if r + 1 < n_units:
                    sort(units[r + 1])
                if new_weight:
                    quantise_weight(units[r][1])
